import numpy as np
import ml_dtypes


def mxq(x, axis, fmt="e4m3"):
    dtype, down = {"e4m3": (ml_dtypes.float8_e4m3fn, 7), "e5m2": (ml_dtypes.float8_e5m2, 14)}[fmt]
    v = np.moveaxis(np.asarray(x, np.float32).astype(ml_dtypes.bfloat16).astype(np.float64), axis, -1)
    blocks = v.reshape(v.shape[:-1] + (-1, 32))
    amax = np.abs(blocks).max(-1, keepdims=True)
    byte = np.maximum(np.where(amax > 0, np.frexp(amax)[1] - 1 + 127, 0) - down, 1)
    scale = np.exp2(byte - 127.0)
    codes = (blocks / scale).astype(np.float32).astype(dtype).astype(np.float64)
    return np.moveaxis((codes * scale).reshape(v.shape), -1, axis)


WIDE = False


def mx_kscale(k):
    if not WIDE:
        return np.ones(k)
    levels = np.array([10, -10, 5, -5, 0])
    if k % 512:
        return np.exp2(np.random.permutation(np.resize(levels, k // 32))).repeat(32)
    a = np.empty((k // 512, 16))
    for p in range(k // 512):
        a[p, :8] = np.random.permutation(np.resize(levels, 8))
        for g in range(8):
            far = levels[np.abs(levels - a[p, g]) >= 10]
            a[p, g + 8] = far[np.random.randint(len(far))]
    return np.exp2(a.ravel()).repeat(32)


BF16 = ml_dtypes.bfloat16


def bf(x):
    return np.asarray(x, np.float32).astype(BF16)


def f64(x):
    return np.asarray(x).astype(np.float64)


B, C, CK, H, W = 2, 1024, 512, 32, 32
N = H * W


def setup_inputs():
    s, t = mx_kscale(C), mx_kscale(CK)
    return {
        "x": bf(np.random.standard_normal((B, C, H, W)) * s[None, :, None, None]),
        "Wq": bf(np.random.standard_normal((CK, C)) / np.sqrt(C) / s[None, :] * t[:, None]),
        "bq": bf(np.random.standard_normal(CK) * 0.3 * t),
        "Wk": bf(np.random.standard_normal((CK, C)) / np.sqrt(C) / s[None, :] / t[:, None]),
        "bk": bf(np.random.standard_normal(CK) * 0.3 / t),
        "fg_sim": bf(np.random.uniform(size=(B, N, N))),
    }


def reference(x, Wq, bq, Wk, bk, fg_sim):
    xq = mxq(f64(x).reshape(B, C, N), 1, "e4m3")
    query = (mxq(f64(Wq), 1, "e4m3") @ xq).transpose(0, 2, 1) + f64(bq)
    key = (mxq(f64(Wk), 1, "e4m3") @ xq) + f64(bk)[None, :, None]
    sim = (mxq(query, 2, "e4m3") @ mxq(key, 1, "e4m3")) * CK ** -0.5
    return sim * f64(fg_sim)

@@ -1,0 +1,255 @@
+from contextlib import ExitStack
+
+import concourse.mybir as mybir
+from concourse.masks import make_identity
+
+F32 = mybir.dt.float32
+BF16 = mybir.dt.bfloat16
+U32 = mybir.dt.uint32
+U8 = mybir.dt.uint8
+FP8X4 = mybir.dt.float8_e4m3fn_x4
+ACT = mybir.ActivationFunctionType
+ALU = mybir.AluOpType
+
+P = 128
+B, C, CK, N = 2, 1024, 512, 1024
+HALF = 512
+FLOPS = 2 * B * (2 * CK * C * N + N * N * CK)
+PINNED = True
+Q = 0
+K = 1
+
+
+def tile_sgan_pa_kernel(tc, x, Wq, bq, Wk, bk, fg_sim, out):
+    nc = tc.nc
+    xf = x.rearrange("b c h w -> b c (h w)")
+    W = [Wq, Wk]
+    bias_dram = [bq, bk]
+
+    with ExitStack() as ctx:
+        if PINNED:
+            ctx.enter_context(tc.manual_schedule())
+        keep = ctx.enter_context(tc.tile_pool(name="keep", bufs=1))
+        big = ctx.enter_context(tc.tile_pool(name="big", bufs=8))
+        stage = ctx.enter_context(tc.tile_pool(name="stage", bufs=4))
+        outp = ctx.enter_context(tc.tile_pool(name="outp", bufs=8))
+        ps1 = ctx.enter_context(tc.psum_pool(name="ps1", bufs=4))
+        ps2 = ctx.enter_context(tc.psum_pool(name="ps2", bufs=4))
+
+        x_raw = {}
+        w_raw = {}
+        fg_sb = {}
+
+        def load_x(b, g):
+            t = big.tile([P, 4 * N], BF16, name="xraw", tag="big")
+            nc.sync.dma_start(
+                out=t[:].rearrange("p (j n) -> p j n", j=4),
+                in_=xf[b, HALF * g:HALF * (g + 1), :].rearrange("(q j) n -> q j n", j=4),
+            )
+            x_raw[(b, g)] = t
+
+        def load_w(w):
+            t = big.tile([P, 4 * C], BF16, name="wraw", tag="big")
+            nc.sync.dma_start(
+                out=t[:].rearrange("p (t c) -> p t c", t=4),
+                in_=W[w].rearrange("(p t) c -> p t c", t=4),
+            )
+            w_raw[w] = t
+
+        def load_fg(b, r):
+            t = big.tile([P, 4 * N], BF16, name="fg", tag="big")
+            nc.sync.dma_start(
+                out=t[:].rearrange("p (i m) -> p i m", i=4),
+                in_=fg_sim[b, HALF * r:HALF * (r + 1), :].rearrange("(a i) m -> a i m", i=4),
+            )
+            fg_sb[(b, r)] = t
+
+        bias_bf = []
+        for w in range(2):
+            t = keep.tile([P, 4], BF16, name="biasbf%d" % w)
+            nc.scalar.dma_start(out=t[:], in_=bias_dram[w].rearrange("(p t) -> p t", t=4))
+            bias_bf.append(t)
+
+        load_w(K)
+        load_x(0, 0)
+        load_x(0, 1)
+        load_w(Q)
+        load_x(1, 0)
+        load_x(1, 1)
+        for b in range(B):
+            for r in range(2):
+                load_fg(b, r)
+
+        ident = keep.tile([P, P], F32, name="ident")
+        make_identity(nc, ident[:])
+        bias = []
+        for w in range(2):
+            t = keep.tile([P, 4], F32, name="bias%d" % w)
+            nc.vector.tensor_copy(out=t[:], in_=bias_bf[w][:])
+            bias.append(t)
+
+        def regroup(on_scalar, dst, src):
+            dst_v = dst[:].rearrange("p (c i s) -> p c s i", i=4, s=4)
+            src_v = src.rearrange("p s (c i) -> p c s i", i=4)
+            if on_scalar:
+                nc.scalar.copy(out=dst_v, in_=src_v)
+            else:
+                nc.vector.tensor_copy(out=dst_v, in_=src_v)
+
+        def quantise(name, grouped):
+            codes = keep.tile([P, HALF], U32, name="c_" + name, align_bytes=64)
+            scales = keep.tile([P, HALF], U8, name="s_" + name, align_bytes=64)
+            nc.vector.quantize_mx(out=codes[:].bitcast(FP8X4), scales=scales[:], in_=grouped[:])
+            return codes, scales
+
+        w_grp = {}
+        w_q = {}
+
+        def WU(w, g):
+            w32 = w_raw[w][:].bitcast(F32)
+            grp = stage.tile([P, 4 * HALF], BF16, name="wgrp", tag="wgrp", bufs=2, align_bytes=64)
+            g32 = grp[:].bitcast(F32).rearrange("p (c u) -> p c u", u=2)
+            for tp in range(2):
+                pw = ps1.tile([P, HALF], F32, name="pw", tag="bank1")
+                for tt in range(2):
+                    for u in range(2):
+                        col = 512 * (2 * tp + tt) + 256 * g
+                        nc.tensor.transpose(
+                            pw[:, (2 * tt + u) * P:(2 * tt + u + 1) * P],
+                            w32[:, col + u:col + 256:2],
+                            ident[:],
+                        )
+                nc.scalar.copy(
+                    out=g32[:, 256 * tp:256 * (tp + 1), :].rearrange("p (tt j) u -> p tt j u", tt=2),
+                    in_=pw[:].rearrange("p (tt u j) -> p tt j u", tt=2, u=2),
+                )
+            w_grp[(w, g)] = grp
+
+        def WQ(w, g):
+            w_q[(w, g)] = quantise("w%d%d" % (w, g), w_grp[(w, g)])
+
+        x_grp = {}
+        x_q = {}
+
+        def XR(b, g, h):
+            grp = stage.tile([P, 4 * HALF], BF16, name="xgrp", tag="xgrp", align_bytes=64)
+            src = x_raw[(b, g)][:].rearrange("p (s n) -> p s n", s=4)[:, :, HALF * h:HALF * (h + 1)]
+            regroup(b == 0 and g == 1 and h == 1, grp, src)
+            x_grp[(b, g, h)] = grp
+
+        def XQ(b, g, h):
+            x_q[(b, g, h)] = quantise("x%d%d%d" % (b, g, h), x_grp[(b, g, h)])
+
+        planes = {}
+        s_grp = {}
+        s_q = {}
+
+        def S1(b, w, h):
+            pl = stage.tile([P, 4 * HALF], BF16, name="planes", tag="planes")
+            plv = pl[:].rearrange("p (t n) -> p t n", t=4)
+            for t in range(4):
+                acc = ps1.tile([P, HALF], F32, name="acc1", tag="bank1")
+                for g in range(2):
+                    wc, ws = w_q[(w, g)]
+                    xc, xs = x_q[(b, g, h)]
+                    nc.tensor.matmul_mx(
+                        out=acc[:],
+                        lhsT=wc[:, P * t:P * (t + 1)].bitcast(FP8X4),
+                        lhsT_scale=ws[:, P * t:P * (t + 1)],
+                        rhs=xc[:].bitcast(FP8X4),
+                        rhs_scale=xs[:],
+                        start=(g == 0),
+                        stop=(g == 1),
+                    )
+                if w == Q:
+                    src = acc[:].rearrange("p (a i) -> p i a", i=4)
+                    dst = plv[:, t, :].rearrange("p (i a) -> p i a", i=4)
+                else:
+                    src = acc[:]
+                    dst = plv[:, t, :]
+                nc.scalar.activation(out=dst, in_=src, func=ACT.Identity, bias=bias[w][:, t:t + 1], scale=1.0)
+            planes[(b, w, h)] = pl
+
+        def RR(b, w, h):
+            grp = stage.tile([P, 4 * HALF], BF16, name="sgrp", tag="sgrp", align_bytes=64)
+            regroup(b == 1, grp, planes[(b, w, h)][:].rearrange("p (t n) -> p t n", t=4))
+            s_grp[(b, w, h)] = grp
+
+        def RQ(b, w, h):
+            s_q[(b, w, h)] = quantise("q%d%d%d" % (b, w, h), s_grp[(b, w, h)])
+
+        def S2(b, r, i, hm):
+            o = outp.tile([P, HALF], F32, name="o")
+            qc, qs = s_q[(b, Q, r)]
+            kc, ks = s_q[(b, K, hm)]
+            acc = ps2.tile([P, HALF], F32, name="acc2")
+            nc.tensor.matmul_mx(
+                out=acc[:],
+                lhsT=qc[:, P * i:P * (i + 1)].bitcast(FP8X4),
+                lhsT_scale=qs[:, P * i:P * (i + 1)],
+                rhs=kc[:].bitcast(FP8X4),
+                rhs_scale=ks[:],
+                start=True,
+                stop=True,
+            )
+            nc.vector.scalar_tensor_tensor(
+                out=o[:],
+                in0=acc[:],
+                scalar=CK ** -0.5,
+                in1=fg_sb[(b, r)][:, N * i + HALF * hm:N * i + HALF * (hm + 1)],
+                op0=ALU.mult,
+                op1=ALU.mult,
+            )
+            nc.sync.dma_start(
+                out=out[b, HALF * r:HALF * (r + 1), :].rearrange("(a i) m -> a i m", i=4)[:, i, HALF * hm:HALF * (hm + 1)],
+                in_=o[:],
+            )
+
+        WU(K, 0)
+        WU(K, 1)
+        XR(0, 0, 0)
+        WQ(K, 0)
+        XR(0, 0, 1)
+        WQ(K, 1)
+        XR(0, 1, 0)
+        XR(0, 1, 1)
+        XQ(0, 0, 0)
+        XQ(0, 1, 0)
+        XQ(0, 0, 1)
+        XQ(0, 1, 1)
+        WU(Q, 0)
+        WU(Q, 1)
+        units = [(b, w, h) for b in range(B) for h in range(2) for w in (K, Q)]
+        x1 = [(1, g, h) for h in range(2) for g in range(2)]
+        banks = []
+        for b in range(B):
+            banks += [(4 * b + 1, (b, 0, i, 0)) for i in range(4)]
+            banks += [(4 * b + 2, (b, 0, i, 1)) for i in range(4)]
+            banks += [(4 * b + 3, (b, 1, i, hm)) for i in range(4) for hm in range(2)]
+        issued = [0]
+
+        def stage2(count, quantised):
+            for z in range(count):
+                if issued[0] < len(banks) and banks[issued[0]][0] <= quantised:
+                    S2(*banks[issued[0]][1])
+                    issued[0] += 1
+
+        for k in range(9):
+            if k < 8:
+                S1(*units[k])
+                if units[k][0] == 1:
+                    RR(*units[k])
+            if k == 0:
+                WQ(Q, 0)
+                WQ(Q, 1)
+            if k < 4:
+                XR(*x1[k])
+            if 1 <= k <= 4:
+                RR(*units[k - 1])
+                XQ(*x1[k - 1])
+            if k == 8:
+                stage2(2, 6)
+            if k >= 1:
+                RQ(*units[k - 1])
+            if k >= 3:
+                stage2(4 if k < 8 else 32, k - 1)

@@ -15,7 +15,6 @@ P = 128
 B, C, CK, N = 2, 1024, 512, 1024
 HALF = 512
 FLOPS = 2 * B * (2 * CK * C * N + N * N * CK)
-PINNED = True
 Q = 0
 K = 1
 
@@ -27,29 +26,33 @@ def tile_sgan_pa_kernel(tc, x, Wq, bq, Wk, bk, fg_sim, out):
     bias_dram = [bq, bk]
 
     with ExitStack() as ctx:
-        if PINNED:
-            ctx.enter_context(tc.manual_schedule())
+        ctx.enter_context(tc.manual_schedule())
         keep = ctx.enter_context(tc.tile_pool(name="keep", bufs=1))
-        big = ctx.enter_context(tc.tile_pool(name="big", bufs=8))
+        big = ctx.enter_context(tc.tile_pool(name="big", bufs=4))
         stage = ctx.enter_context(tc.tile_pool(name="stage", bufs=4))
-        outp = ctx.enter_context(tc.tile_pool(name="outp", bufs=8))
+        outp = ctx.enter_context(tc.tile_pool(name="outp", bufs=12))
         ps1 = ctx.enter_context(tc.psum_pool(name="ps1", bufs=4))
         ps2 = ctx.enter_context(tc.psum_pool(name="ps2", bufs=4))
 
-        x_raw = {}
+        x_half = {}
         w_raw = {}
         fg_sb = {}
 
+        def load_x_half(b, g, h):
+            t = keep.tile([P, 4 * HALF], BF16, name="xh%d%d%d" % (b, g, h))
+            tv = t[:].rearrange("p (j n) -> p j n", j=4)
+            nc.sync.dma_start(out=tv, in_=xf[b, HALF * g:HALF * (g + 1), HALF * h:HALF * (h + 1)].rearrange("(q j) n -> q j n", j=4))
+            x_half[(b, g, h)] = tv
+
         def load_x(b, g):
-            t = big.tile([P, 4 * N], BF16, name="xraw", tag="big")
-            nc.sync.dma_start(
-                out=t[:].rearrange("p (j n) -> p j n", j=4),
-                in_=xf[b, HALF * g:HALF * (g + 1), :].rearrange("(q j) n -> q j n", j=4),
-            )
-            x_raw[(b, g)] = t
+            t = keep.tile([P, 4 * N], BF16, name="x%d%d" % (b, g))
+            tv = t[:].rearrange("p (j n) -> p j n", j=4)
+            nc.sync.dma_start(out=tv, in_=xf[b, HALF * g:HALF * (g + 1), :].rearrange("(q j) n -> q j n", j=4))
+            for h in range(2):
+                x_half[(b, g, h)] = tv[:, :, HALF * h:HALF * (h + 1)]
 
         def load_w(w):
-            t = big.tile([P, 4 * C], BF16, name="wraw", tag="big")
+            t = keep.tile([P, 4 * C], BF16, name="wraw%d" % w)
             nc.sync.dma_start(
                 out=t[:].rearrange("p (t c) -> p t c", t=4),
                 in_=W[w].rearrange("(p t) c -> p t c", t=4),
@@ -57,7 +60,7 @@ def tile_sgan_pa_kernel(tc, x, Wq, bq, Wk, bk, fg_sim, out):
             w_raw[w] = t
 
         def load_fg(b, r):
-            t = big.tile([P, 4 * N], BF16, name="fg", tag="big")
+            t = big.tile([P, 4 * N], BF16, name="fg", tag="fg")
             nc.sync.dma_start(
                 out=t[:].rearrange("p (i m) -> p i m", i=4),
                 in_=fg_sim[b, HALF * r:HALF * (r + 1), :].rearrange("(a i) m -> a i m", i=4),
@@ -70,28 +73,45 @@ def tile_sgan_pa_kernel(tc, x, Wq, bq, Wk, bk, fg_sim, out):
             nc.scalar.dma_start(out=t[:], in_=bias_dram[w].rearrange("(p t) -> p t", t=4))
             bias_bf.append(t)
 
+        load_x_half(0, 0, 0)
+        load_x_half(0, 1, 0)
+        load_x_half(0, 0, 1)
+        load_x_half(0, 1, 1)
         load_w(K)
-        load_x(0, 0)
-        load_x(0, 1)
+        load_x_half(1, 0, 0)
+        load_x_half(1, 1, 0)
         load_w(Q)
-        load_x(1, 0)
-        load_x(1, 1)
+        load_x_half(1, 0, 1)
+        load_x_half(1, 1, 1)
         for b in range(B):
             for r in range(2):
                 load_fg(b, r)
 
         ident = keep.tile([P, P], F32, name="ident")
         make_identity(nc, ident[:])
-        bias = []
-        for w in range(2):
-            t = keep.tile([P, 4], F32, name="bias%d" % w)
-            nc.vector.tensor_copy(out=t[:], in_=bias_bf[w][:])
-            bias.append(t)
+        identb = keep.tile([P, P], BF16, name="identb")
+        nc.gpsimd.tensor_copy(out=identb[:], in_=ident[:])
 
-        def regroup(on_scalar, dst, src):
+        def regroup(how, dst, src):
+            if how == "P":
+                for z in range(2):
+                    pb = ps1.tile([P, 2 * HALF], BF16, name="pb", tag="bank1")
+                    for y in range(2):
+                        c0 = 256 * z + P * y
+                        nc.tensor.matmul(pb[:, HALF * y:HALF * (y + 1)], identb[:], src[:, :, c0:c0 + P].rearrange("p s c -> p c s"), start=True, stop=True)
+                    nc.scalar.copy(out=dst[:, 1024 * z:1024 * (z + 1)], in_=pb[:])
+                return
             dst_v = dst[:].rearrange("p (c i s) -> p c s i", i=4, s=4)
             src_v = src.rearrange("p s (c i) -> p c s i", i=4)
-            if on_scalar:
+            if how[0] == "X":
+                cv = int(how[1:])
+                dv, sv = dst[:].rearrange("p (c i s) -> p c s i", i=4, s=4), src.rearrange("p s (c i) -> p c s i", i=4)
+                nc.vector.tensor_copy(out=dv[:, :cv // 4], in_=sv[:, :cv // 4])
+                nc.scalar.copy(out=dv[:, cv // 4:], in_=sv[:, cv // 4:])
+            elif how == "G":
+                for z in range(4):
+                    nc.gpsimd.tensor_scalar(out=dst[:, 512 * z:512 * (z + 1)].rearrange("p (c i s) -> p c s i", i=4, s=4), in0=src[:, :, P * z:P * (z + 1)].rearrange("p s (c i) -> p c s i", i=4), scalar1=1.0, scalar2=0.0, op0=ALU.mult, op1=ALU.add)
+            elif how == "S":
                 nc.scalar.copy(out=dst_v, in_=src_v)
             else:
                 nc.vector.tensor_copy(out=dst_v, in_=src_v)
@@ -131,10 +151,9 @@ def tile_sgan_pa_kernel(tc, x, Wq, bq, Wk, bk, fg_sim, out):
         x_grp = {}
         x_q = {}
 
-        def XR(b, g, h):
+        def XR(b, g, h, how="V"):
             grp = stage.tile([P, 4 * HALF], BF16, name="xgrp", tag="xgrp", align_bytes=64)
-            src = x_raw[(b, g)][:].rearrange("p (s n) -> p s n", s=4)[:, :, HALF * h:HALF * (h + 1)]
-            regroup(b == 0 and g == 1 and h == 1, grp, src)
+            regroup(how, grp, x_half[(b, g, h)])
             x_grp[(b, g, h)] = grp
 
         def XQ(b, g, h):
@@ -144,10 +163,12 @@ def tile_sgan_pa_kernel(tc, x, Wq, bq, Wk, bk, fg_sim, out):
         s_grp = {}
         s_q = {}
 
-        def S1(b, w, h):
-            pl = stage.tile([P, 4 * HALF], BF16, name="planes", tag="planes")
-            plv = pl[:].rearrange("p (t n) -> p t n", t=4)
-            for t in range(4):
+        def S1(b, w, h, ts=(0, 1, 2, 3)):
+            if 0 in ts:
+                pl = stage.tile([P, 4 * HALF], BF16, name="planes", tag="planes", bufs=6)
+                planes[(b, w, h)] = pl[:].rearrange("p (t n) -> p t n", t=4)
+            plv = planes[(b, w, h)]
+            for t in ts:
                 acc = ps1.tile([P, HALF], F32, name="acc1", tag="bank1")
                 for g in range(2):
                     wc, ws = w_q[(w, g)]
@@ -167,22 +188,36 @@ def tile_sgan_pa_kernel(tc, x, Wq, bq, Wk, bk, fg_sim, out):
                 else:
                     src = acc[:]
                     dst = plv[:, t, :]
-                nc.scalar.activation(out=dst, in_=src, func=ACT.Identity, bias=bias[w][:, t:t + 1], scale=1.0)
-            planes[(b, w, h)] = pl
+                nc.scalar.activation(out=dst, in_=src, func=ACT.Identity, bias=bias_bf[w][:, t:t + 1], scale=1.0)
 
-        def RR(b, w, h):
+        def RR(b, w, h, how="V"):
             grp = stage.tile([P, 4 * HALF], BF16, name="sgrp", tag="sgrp", align_bytes=64)
-            regroup(b == 1, grp, planes[(b, w, h)][:].rearrange("p (t n) -> p t n", t=4))
+            regroup(how, grp, planes[(b, w, h)])
             s_grp[(b, w, h)] = grp
 
         def RQ(b, w, h):
             s_q[(b, w, h)] = quantise("q%d%d%d" % (b, w, h), s_grp[(b, w, h)])
 
-        def S2(b, r, i, hm):
-            o = outp.tile([P, HALF], F32, name="o")
+        accs = {}
+        late = []
+
+        def store(b, r, i, hm, o):
+            nc.sync.dma_start(
+                out=out[b, HALF * r:HALF * (r + 1), :].rearrange("(a i) m -> a i m", i=4)[:, i, HALF * hm:HALF * (hm + 1)],
+                in_=o[:],
+            )
+
+        def flush():
+            while late:
+                store(*late.pop(0))
+
+        def SM(b, r, i, hm, off=False):
             qc, qs = s_q[(b, Q, r)]
             kc, ks = s_q[(b, K, hm)]
-            acc = ps2.tile([P, HALF], F32, name="acc2")
+            if off:
+                acc = ps1.tile([P, HALF], F32, name="acc3", tag="bank1")
+            else:
+                acc = ps2.tile([P, HALF], F32, name="acc2")
             nc.tensor.matmul_mx(
                 out=acc[:],
                 lhsT=qc[:, P * i:P * (i + 1)].bitcast(FP8X4),
@@ -192,64 +227,115 @@ def tile_sgan_pa_kernel(tc, x, Wq, bq, Wk, bk, fg_sim, out):
                 start=True,
                 stop=True,
             )
-            nc.vector.scalar_tensor_tensor(
-                out=o[:],
-                in0=acc[:],
-                scalar=CK ** -0.5,
-                in1=fg_sb[(b, r)][:, N * i + HALF * hm:N * i + HALF * (hm + 1)],
-                op0=ALU.mult,
-                op1=ALU.mult,
-            )
-            nc.sync.dma_start(
-                out=out[b, HALF * r:HALF * (r + 1), :].rearrange("(a i) m -> a i m", i=4)[:, i, HALF * hm:HALF * (hm + 1)],
-                in_=o[:],
-            )
+            accs[(b, r, i, hm)] = acc
 
-        WU(K, 0)
-        WU(K, 1)
+        def SE(b, r, i, hm, off=False):
+            acc = accs[(b, r, i, hm)]
+            fg = fg_sb[(b, r)][:, N * i + HALF * hm:N * i + HALF * (hm + 1)]
+            if off:
+                o = outp.tile([P, HALF], F32, name="og", bufs=4)
+                sc = stage.tile([P, HALF], F32, name="sc", tag="sc", bufs=4)
+                nc.scalar.activation(out=sc[:], in_=acc[:], func=ACT.Copy, scale=CK ** -0.5)
+                for z in range(2):
+                    cz = slice(256 * z, 256 * (z + 1))
+                    nc.gpsimd.tensor_tensor(out=o[:, cz], in0=sc[:, cz], in1=fg[:, cz], op=ALU.mult)
+            else:
+                o = outp.tile([P, HALF], F32, name="o")
+                nc.vector.scalar_tensor_tensor(out=o[:], in0=acc[:], scalar=CK ** -0.5, in1=fg, op0=ALU.mult, op1=ALU.mult)
+            if off:
+                late.append((b, r, i, hm, o))
+            else:
+                store(b, r, i, hm, o)
+
+        def group(b, r, hm, lo, hi):
+            return [(b, r, i, hm) for i in range(lo, hi)]
+
+        def sm(*t):
+            for u in t:
+                SM(*u)
+
+        def se(*t):
+            for u in t:
+                SE(*u)
+
+        def off(*t):
+            for u in t:
+                SM(*u, off=True)
+                SE(*u, off=True)
+
         XR(0, 0, 0)
-        WQ(K, 0)
-        XR(0, 0, 1)
-        WQ(K, 1)
-        XR(0, 1, 0)
-        XR(0, 1, 1)
+        XR(0, 1, 0, "S")
         XQ(0, 0, 0)
+        XR(0, 0, 1)
+        XR(0, 1, 1, "S")
         XQ(0, 1, 0)
         XQ(0, 0, 1)
         XQ(0, 1, 1)
+        WU(K, 0)
+        WU(K, 1)
+        XR(1, 0, 0)
+        WQ(K, 0)
+        XQ(1, 0, 0)
+        WQ(K, 1)
+        S1(0, K, 0)
+        XR(1, 1, 0)
+        XQ(1, 1, 0)
         WU(Q, 0)
         WU(Q, 1)
-        units = [(b, w, h) for b in range(B) for h in range(2) for w in (K, Q)]
-        x1 = [(1, g, h) for h in range(2) for g in range(2)]
-        banks = []
-        for b in range(B):
-            banks += [(4 * b + 1, (b, 0, i, 0)) for i in range(4)]
-            banks += [(4 * b + 2, (b, 0, i, 1)) for i in range(4)]
-            banks += [(4 * b + 3, (b, 1, i, hm)) for i in range(4) for hm in range(2)]
-        issued = [0]
+        S1(0, K, 1)
+        XR(1, 0, 1)
+        XR(1, 1, 1)
+        RR(0, K, 0)
+        WQ(Q, 0)
+        WQ(Q, 1)
+        RQ(0, K, 0)
+        XQ(1, 0, 1)
+        S1(0, Q, 0)
+        XQ(1, 1, 1)
+        RR(0, K, 1)
+        S1(0, Q, 1)
+        RQ(0, K, 1)
+        RR(0, Q, 0)
+        S1(1, K, 0)
+        RQ(0, Q, 0)
+        RR(0, Q, 1)
+        g = [group(b, r, h, 0, 4) for b in range(2) for r in range(2) for h in range(2)]
 
-        def stage2(count, quantised):
-            for z in range(count):
-                if issued[0] < len(banks) and banks[issued[0]][0] <= quantised:
-                    S2(*banks[issued[0]][1])
-                    issued[0] += 1
+        def both(*t):
+            for u in t:
+                SM(*u)
+                SE(*u)
 
-        for k in range(9):
-            if k < 8:
-                S1(*units[k])
-                if units[k][0] == 1:
-                    RR(*units[k])
-            if k == 0:
-                WQ(Q, 0)
-                WQ(Q, 1)
-            if k < 4:
-                XR(*x1[k])
-            if 1 <= k <= 4:
-                RR(*units[k - 1])
-                XQ(*x1[k - 1])
-            if k == 8:
-                stage2(2, 6)
-            if k >= 1:
-                RQ(*units[k - 1])
-            if k >= 3:
-                stage2(4 if k < 8 else 32, k - 1)
+        sm(*g[0])
+        se(*g[0][:2])
+        RQ(0, Q, 1)
+        S1(1, Q, 0)
+        se(*g[0][2:])
+        RR(1, Q, 0, "S")
+        sm(*g[1])
+        RR(1, K, 0)
+        se(*g[1][:2])
+        RQ(1, K, 0)
+        se(*g[1][2:])
+        S1(1, K, 1)
+        sm(*g[2])
+        RR(1, K, 1, "S")
+        se(*g[2])
+        RQ(1, Q, 0)
+        sm(*g[3])
+        S1(1, Q, 1)
+        se(*g[3][:2])
+        RR(1, Q, 1, "S")
+        sm(*g[4][:2])
+        se(*g[3][2:])
+        RQ(1, K, 1)
+        sm(*g[4][2:])
+        se(*g[4][:2])
+        sm(*g[5][:2])
+        se(*g[4][2:])
+        sm(*g[5][2:])
+        se(*g[5][:2])
+        RQ(1, Q, 1)
+        se(*g[5][2:])
+        both(*g[6])
+        both(*g[7])

@@ -73,16 +73,12 @@ def tile_sgan_pa_kernel(tc, x, Wq, bq, Wk, bk, fg_sim, out):
             nc.scalar.dma_start(out=t[:], in_=bias_dram[w].rearrange("(p t) -> p t", t=4))
             bias_bf.append(t)
 
-        load_x_half(0, 0, 0)
-        load_x_half(0, 1, 0)
-        load_x_half(0, 0, 1)
-        load_x_half(0, 1, 1)
+        load_x(0, 0)
+        load_x(0, 1)
         load_w(K)
-        load_x_half(1, 0, 0)
-        load_x_half(1, 1, 0)
+        load_x(1, 0)
         load_w(Q)
-        load_x_half(1, 0, 1)
-        load_x_half(1, 1, 1)
+        load_x(1, 1)
         for b in range(B):
             for r in range(2):
                 load_fg(b, r)
@@ -264,35 +260,35 @@ def tile_sgan_pa_kernel(tc, x, Wq, bq, Wk, bk, fg_sim, out):
                 SE(*u, off=True)
 
         XR(0, 0, 0)
-        XR(0, 1, 0, "S")
+        XR(0, 0, 1, "S")
         XQ(0, 0, 0)
-        XR(0, 0, 1)
+        XR(0, 1, 0)
         XR(0, 1, 1, "S")
-        XQ(0, 1, 0)
         XQ(0, 0, 1)
+        XQ(0, 1, 0)
         XQ(0, 1, 1)
         WU(K, 0)
         WU(K, 1)
         XR(1, 0, 0)
         WQ(K, 0)
-        XQ(1, 0, 0)
         WQ(K, 1)
         S1(0, K, 0)
-        XR(1, 1, 0)
-        XQ(1, 1, 0)
+        XR(1, 0, 1)
+        XQ(1, 0, 0)
         WU(Q, 0)
         WU(Q, 1)
         S1(0, K, 1)
-        XR(1, 0, 1)
-        XR(1, 1, 1)
+        XQ(1, 0, 1)
+        XR(1, 1, 0)
         RR(0, K, 0)
         WQ(Q, 0)
         WQ(Q, 1)
         RQ(0, K, 0)
-        XQ(1, 0, 1)
+        XQ(1, 1, 0)
         S1(0, Q, 0)
-        XQ(1, 1, 1)
+        XR(1, 1, 1)
         RR(0, K, 1)
+        XQ(1, 1, 1)
         S1(0, Q, 1)
         RQ(0, K, 1)
         RR(0, Q, 0)

@@ -195,6 +195,8 @@ def tile_sgan_pa_kernel(tc, x, Wq, bq, Wk, bk, fg_sim, out):
             s_q[(b, w, h)] = quantise("q%d%d%d" % (b, w, h), s_grp[(b, w, h)])
 
         accs = {}
+        pairs = {}
+        PAIR = {(0, 0): True, (0, 1): True, (1, 0): False, (1, 1): True}
         late = []
 
         def store(b, r, i, hm, o):
@@ -235,8 +237,16 @@ def tile_sgan_pa_kernel(tc, x, Wq, bq, Wk, bk, fg_sim, out):
                 for z in range(2):
                     cz = slice(256 * z, 256 * (z + 1))
                     nc.gpsimd.tensor_tensor(out=o[:, cz], in0=sc[:, cz], in1=fg[:, cz], op=ALU.mult)
+            elif PAIR[(b, r)]:
+                if hm == 0:
+                    pairs[(b, r, i)] = outp.tile([P, 2 * HALF], F32, name="o2", bufs=8)
+                o2 = pairs[(b, r, i)]
+                nc.vector.scalar_tensor_tensor(out=o2[:, HALF * hm:HALF * (hm + 1)], in0=acc[:], scalar=CK ** -0.5, in1=fg, op0=ALU.mult, op1=ALU.mult)
+                if hm == 1:
+                    nc.sync.dma_start(out=out[b, HALF * r:HALF * (r + 1), :].rearrange("(a i) m -> a i m", i=4)[:, i, :], in_=o2[:])
+                return
             else:
-                o = outp.tile([P, HALF], F32, name="o")
+                o = outp.tile([P, HALF], F32, name="o", bufs=4)
                 nc.vector.scalar_tensor_tensor(out=o[:], in0=acc[:], scalar=CK ** -0.5, in1=fg, op0=ALU.mult, op1=ALU.mult)
             if off:
                 late.append((b, r, i, hm, o))
@@ -294,14 +304,18 @@ def tile_sgan_pa_kernel(tc, x, Wq, bq, Wk, bk, fg_sim, out):
         RR(0, Q, 0)
         S1(1, K, 0)
         RQ(0, Q, 0)
-        RR(0, Q, 1)
         g = [group(b, r, h, 0, 4) for b in range(2) for r in range(2) for h in range(2)]
+        for z in (0, 2, 6):
+            b, r = g[z][0][:2]
+            p = [(b, r, i, h) for i in range(4) for h in range(2)]
+            g[z], g[z + 1] = p[:4], p[4:]
 
         def both(*t):
             for u in t:
                 SM(*u)
                 SE(*u)
 
+        RR(0, Q, 1)
         sm(*g[0])
         se(*g[0][:2])
         RQ(0, Q, 1)

from contextlib import ExitStack

import concourse.mybir as mybir
from concourse.masks import make_identity

F32 = mybir.dt.float32
BF16 = mybir.dt.bfloat16
U32 = mybir.dt.uint32
U8 = mybir.dt.uint8
FP8X4 = mybir.dt.float8_e4m3fn_x4
ACT = mybir.ActivationFunctionType
ALU = mybir.AluOpType

P = 128
B, C, CK, N = 2, 1024, 512, 1024
HALF = 512
FLOPS = 2 * B * (2 * CK * C * N + N * N * CK)
Q = 0
K = 1


def tile_sgan_pa_kernel(tc, x, Wq, bq, Wk, bk, fg_sim, out):
    nc = tc.nc
    xf = x.rearrange("b c h w -> b c (h w)")
    W = [Wq, Wk]
    bias_dram = [bq, bk]

    with ExitStack() as ctx:
        ctx.enter_context(tc.manual_schedule())
        keep = ctx.enter_context(tc.tile_pool(name="keep", bufs=1))
        big = ctx.enter_context(tc.tile_pool(name="big", bufs=4))
        stage = ctx.enter_context(tc.tile_pool(name="stage", bufs=4))
        outp = ctx.enter_context(tc.tile_pool(name="outp", bufs=12))
        ps1 = ctx.enter_context(tc.psum_pool(name="ps1", bufs=4))
        ps2 = ctx.enter_context(tc.psum_pool(name="ps2", bufs=4))

        x_half = {}
        w_raw = {}
        fg_sb = {}

        def load_x_half(b, g, h):
            t = keep.tile([P, 4 * HALF], BF16, name="xh%d%d%d" % (b, g, h))
            tv = t[:].rearrange("p (j n) -> p j n", j=4)
            nc.sync.dma_start(out=tv, in_=xf[b, HALF * g:HALF * (g + 1), HALF * h:HALF * (h + 1)].rearrange("(q j) n -> q j n", j=4))
            x_half[(b, g, h)] = tv

        def load_x(b, g):
            t = keep.tile([P, 4 * N], BF16, name="x%d%d" % (b, g))
            tv = t[:].rearrange("p (j n) -> p j n", j=4)
            nc.sync.dma_start(out=tv, in_=xf[b, HALF * g:HALF * (g + 1), :].rearrange("(q j) n -> q j n", j=4))
            for h in range(2):
                x_half[(b, g, h)] = tv[:, :, HALF * h:HALF * (h + 1)]

        def load_w(w):
            t = keep.tile([P, 4 * C], BF16, name="wraw%d" % w)
            nc.sync.dma_start(
                out=t[:].rearrange("p (t c) -> p t c", t=4),
                in_=W[w].rearrange("(p t) c -> p t c", t=4),
            )
            w_raw[w] = t

        def load_fg(b, r):
            t = big.tile([P, 4 * N], BF16, name="fg", tag="fg")
            nc.sync.dma_start(
                out=t[:].rearrange("p (i m) -> p i m", i=4),
                in_=fg_sim[b, HALF * r:HALF * (r + 1), :].rearrange("(a i) m -> a i m", i=4),
            )
            fg_sb[(b, r)] = t

        bias_bf = []
        for w in range(2):
            t = keep.tile([P, 4], BF16, name="biasbf%d" % w)
            nc.scalar.dma_start(out=t[:], in_=bias_dram[w].rearrange("(p t) -> p t", t=4))
            bias_bf.append(t)

        load_x(0, 0)
        load_x(0, 1)
        load_w(K)
        load_x(1, 0)
        load_w(Q)
        load_x(1, 1)
        for b in range(B):
            for r in range(2):
                load_fg(b, r)

        ident = keep.tile([P, P], F32, name="ident")
        make_identity(nc, ident[:])
        identb = keep.tile([P, P], BF16, name="identb")
        nc.gpsimd.tensor_copy(out=identb[:], in_=ident[:])

        def regroup(how, dst, src):
            if how == "P":
                for z in range(2):
                    pb = ps1.tile([P, 2 * HALF], BF16, name="pb", tag="bank1")
                    for y in range(2):
                        c0 = 256 * z + P * y
                        nc.tensor.matmul(pb[:, HALF * y:HALF * (y + 1)], identb[:], src[:, :, c0:c0 + P].rearrange("p s c -> p c s"), start=True, stop=True)
                    nc.scalar.copy(out=dst[:, 1024 * z:1024 * (z + 1)], in_=pb[:])
                return
            dst_v = dst[:].rearrange("p (c i s) -> p c s i", i=4, s=4)
            src_v = src.rearrange("p s (c i) -> p c s i", i=4)
            if how[0] == "X":
                cv = int(how[1:])
                dv, sv = dst[:].rearrange("p (c i s) -> p c s i", i=4, s=4), src.rearrange("p s (c i) -> p c s i", i=4)
                nc.vector.tensor_copy(out=dv[:, :cv // 4], in_=sv[:, :cv // 4])
                nc.scalar.copy(out=dv[:, cv // 4:], in_=sv[:, cv // 4:])
            elif how == "G":
                for z in range(4):
                    nc.gpsimd.tensor_scalar(out=dst[:, 512 * z:512 * (z + 1)].rearrange("p (c i s) -> p c s i", i=4, s=4), in0=src[:, :, P * z:P * (z + 1)].rearrange("p s (c i) -> p c s i", i=4), scalar1=1.0, scalar2=0.0, op0=ALU.mult, op1=ALU.add)
            elif how == "S":
                nc.scalar.copy(out=dst_v, in_=src_v)
            else:
                nc.vector.tensor_copy(out=dst_v, in_=src_v)

        def quantise(name, grouped):
            codes = keep.tile([P, HALF], U32, name="c_" + name, align_bytes=64)
            scales = keep.tile([P, HALF], U8, name="s_" + name, align_bytes=64)
            nc.vector.quantize_mx(out=codes[:].bitcast(FP8X4), scales=scales[:], in_=grouped[:])
            return codes, scales

        w_grp = {}
        w_q = {}

        def WU(w, g):
            w32 = w_raw[w][:].bitcast(F32)
            grp = stage.tile([P, 4 * HALF], BF16, name="wgrp", tag="wgrp", bufs=2, align_bytes=64)
            g32 = grp[:].bitcast(F32).rearrange("p (c u) -> p c u", u=2)
            for tp in range(2):
                pw = ps1.tile([P, HALF], F32, name="pw", tag="bank1")
                for tt in range(2):
                    for u in range(2):
                        col = 512 * (2 * tp + tt) + 256 * g
                        nc.tensor.transpose(
                            pw[:, (2 * tt + u) * P:(2 * tt + u + 1) * P],
                            w32[:, col + u:col + 256:2],
                            ident[:],
                        )
                nc.scalar.copy(
                    out=g32[:, 256 * tp:256 * (tp + 1), :].rearrange("p (tt j) u -> p tt j u", tt=2),
                    in_=pw[:].rearrange("p (tt u j) -> p tt j u", tt=2, u=2),
                )
            w_grp[(w, g)] = grp

        def WQ(w, g):
            w_q[(w, g)] = quantise("w%d%d" % (w, g), w_grp[(w, g)])

        x_grp = {}
        x_q = {}

        def XR(b, g, h, how="V"):
            grp = stage.tile([P, 4 * HALF], BF16, name="xgrp", tag="xgrp", align_bytes=64)
            regroup(how, grp, x_half[(b, g, h)])
            x_grp[(b, g, h)] = grp

        def XQ(b, g, h):
            x_q[(b, g, h)] = quantise("x%d%d%d" % (b, g, h), x_grp[(b, g, h)])

        planes = {}
        s_grp = {}
        s_q = {}

        def S1(b, w, h, ts=(0, 1, 2, 3)):
            if 0 in ts:
                pl = stage.tile([P, 4 * HALF], BF16, name="planes", tag="planes", bufs=6)
                planes[(b, w, h)] = pl[:].rearrange("p (t n) -> p t n", t=4)
            plv = planes[(b, w, h)]
            for t in ts:
                acc = ps1.tile([P, HALF], F32, name="acc1", tag="bank1")
                for g in range(2):
                    wc, ws = w_q[(w, g)]
                    xc, xs = x_q[(b, g, h)]
                    nc.tensor.matmul_mx(
                        out=acc[:],
                        lhsT=wc[:, P * t:P * (t + 1)].bitcast(FP8X4),
                        lhsT_scale=ws[:, P * t:P * (t + 1)],
                        rhs=xc[:].bitcast(FP8X4),
                        rhs_scale=xs[:],
                        start=(g == 0),
                        stop=(g == 1),
                    )
                if w == Q:
                    src = acc[:].rearrange("p (a i) -> p i a", i=4)
                    dst = plv[:, t, :].rearrange("p (i a) -> p i a", i=4)
                else:
                    src = acc[:]
                    dst = plv[:, t, :]
                nc.scalar.activation(out=dst, in_=src, func=ACT.Identity, bias=bias_bf[w][:, t:t + 1], scale=1.0)

        def RR(b, w, h, how="V"):
            grp = stage.tile([P, 4 * HALF], BF16, name="sgrp", tag="sgrp", align_bytes=64)
            regroup(how, grp, planes[(b, w, h)])
            s_grp[(b, w, h)] = grp

        def RQ(b, w, h):
            s_q[(b, w, h)] = quantise("q%d%d%d" % (b, w, h), s_grp[(b, w, h)])

        accs = {}
        pairs = {}
        PAIR = {(0, 0): True, (0, 1): True, (1, 0): False, (1, 1): True}
        late = []

        def store(b, r, i, hm, o):
            nc.sync.dma_start(
                out=out[b, HALF * r:HALF * (r + 1), :].rearrange("(a i) m -> a i m", i=4)[:, i, HALF * hm:HALF * (hm + 1)],
                in_=o[:],
            )

        def flush():
            while late:
                store(*late.pop(0))

        def SM(b, r, i, hm, off=False):
            qc, qs = s_q[(b, Q, r)]
            kc, ks = s_q[(b, K, hm)]
            if off:
                acc = ps1.tile([P, HALF], F32, name="acc3", tag="bank1")
            else:
                acc = ps2.tile([P, HALF], F32, name="acc2")
            nc.tensor.matmul_mx(
                out=acc[:],
                lhsT=qc[:, P * i:P * (i + 1)].bitcast(FP8X4),
                lhsT_scale=qs[:, P * i:P * (i + 1)],
                rhs=kc[:].bitcast(FP8X4),
                rhs_scale=ks[:],
                start=True,
                stop=True,
            )
            accs[(b, r, i, hm)] = acc

        def SE(b, r, i, hm, off=False):
            acc = accs[(b, r, i, hm)]
            fg = fg_sb[(b, r)][:, N * i + HALF * hm:N * i + HALF * (hm + 1)]
            if off:
                o = outp.tile([P, HALF], F32, name="og", bufs=4)
                sc = stage.tile([P, HALF], F32, name="sc", tag="sc", bufs=4)
                nc.scalar.activation(out=sc[:], in_=acc[:], func=ACT.Copy, scale=CK ** -0.5)
                for z in range(2):
                    cz = slice(256 * z, 256 * (z + 1))
                    nc.gpsimd.tensor_tensor(out=o[:, cz], in0=sc[:, cz], in1=fg[:, cz], op=ALU.mult)
            elif PAIR[(b, r)]:
                if hm == 0:
                    pairs[(b, r, i)] = outp.tile([P, 2 * HALF], F32, name="o2", bufs=8)
                o2 = pairs[(b, r, i)]
                nc.vector.scalar_tensor_tensor(out=o2[:, HALF * hm:HALF * (hm + 1)], in0=acc[:], scalar=CK ** -0.5, in1=fg, op0=ALU.mult, op1=ALU.mult)
                if hm == 1:
                    nc.sync.dma_start(out=out[b, HALF * r:HALF * (r + 1), :].rearrange("(a i) m -> a i m", i=4)[:, i, :], in_=o2[:])
                return
            else:
                o = outp.tile([P, HALF], F32, name="o", bufs=4)
                nc.vector.scalar_tensor_tensor(out=o[:], in0=acc[:], scalar=CK ** -0.5, in1=fg, op0=ALU.mult, op1=ALU.mult)
            if off:
                late.append((b, r, i, hm, o))
            else:
                store(b, r, i, hm, o)

        def group(b, r, hm, lo, hi):
            return [(b, r, i, hm) for i in range(lo, hi)]

        def sm(*t):
            for u in t:
                SM(*u)

        def se(*t):
            for u in t:
                SE(*u)

        def off(*t):
            for u in t:
                SM(*u, off=True)
                SE(*u, off=True)

        XR(0, 0, 0)
        XR(0, 0, 1, "S")
        XQ(0, 0, 0)
        XR(0, 1, 0)
        XR(0, 1, 1, "S")
        XQ(0, 0, 1)
        XQ(0, 1, 0)
        XQ(0, 1, 1)
        WU(K, 0)
        WU(K, 1)
        XR(1, 0, 0)
        WQ(K, 0)
        WQ(K, 1)
        S1(0, K, 0)
        XR(1, 0, 1)
        XQ(1, 0, 0)
        WU(Q, 0)
        WU(Q, 1)
        S1(0, K, 1)
        XQ(1, 0, 1)
        XR(1, 1, 0)
        RR(0, K, 0)
        WQ(Q, 0)
        WQ(Q, 1)
        RQ(0, K, 0)
        XQ(1, 1, 0)
        S1(0, Q, 0)
        XR(1, 1, 1)
        RR(0, K, 1)
        XQ(1, 1, 1)
        S1(0, Q, 1)
        RQ(0, K, 1)
        RR(0, Q, 0)
        S1(1, K, 0)
        RQ(0, Q, 0)
        g = [group(b, r, h, 0, 4) for b in range(2) for r in range(2) for h in range(2)]
        for z in (0, 2, 6):
            b, r = g[z][0][:2]
            p = [(b, r, i, h) for i in range(4) for h in range(2)]
            g[z], g[z + 1] = p[:4], p[4:]

        def both(*t):
            for u in t:
                SM(*u)
                SE(*u)

        RR(0, Q, 1)
        sm(*g[0])
        se(*g[0][:2])
        RQ(0, Q, 1)
        S1(1, Q, 0)
        se(*g[0][2:])
        RR(1, Q, 0, "S")
        sm(*g[1])
        RR(1, K, 0)
        se(*g[1][:2])
        RQ(1, K, 0)
        se(*g[1][2:])
        S1(1, K, 1)
        sm(*g[2])
        RR(1, K, 1, "S")
        se(*g[2])
        RQ(1, Q, 0)
        sm(*g[3])
        S1(1, Q, 1)
        se(*g[3][:2])
        RR(1, Q, 1, "S")
        sm(*g[4][:2])
        se(*g[3][2:])
        RQ(1, K, 1)
        sm(*g[4][2:])
        se(*g[4][:2])
        sm(*g[5][:2])
        se(*g[4][2:])
        sm(*g[5][2:])
        se(*g[5][:2])
        RQ(1, Q, 1)
        se(*g[5][2:])
        both(*g[6])
        both(*g[7])
